import numpy as np
import ml_dtypes


def mxq(x, axis, fmt="e4m3"):
    dtype, down = {"e4m3": (ml_dtypes.float8_e4m3fn, 7), "e5m2": (ml_dtypes.float8_e5m2, 14)}[fmt]
    v = np.moveaxis(np.asarray(x, np.float32).astype(ml_dtypes.bfloat16).astype(np.float64), axis, -1)
    blocks = v.reshape(v.shape[:-1] + (-1, 32))
    amax = np.abs(blocks).max(-1, keepdims=True)
    byte = np.maximum(np.where(amax > 0, np.frexp(amax)[1] - 1 + 127, 0) - down, 1)
    scale = np.exp2(byte - 127.0)
    codes = (blocks / scale).astype(np.float32).astype(dtype).astype(np.float64)
    return np.moveaxis((codes * scale).reshape(v.shape), -1, axis)


WIDE = False


def mx_kscale(k):
    if not WIDE:
        return np.ones(k)
    levels = np.array([10, -10, 5, -5, 0])
    a = np.random.permutation(np.resize(levels, k // 512 * 4)).reshape(k // 512, 4)
    idx = np.arange(k)
    return np.exp2(a[idx // 512, idx % 128 // 32])


BF16 = ml_dtypes.bfloat16


def bf(x):
    return np.asarray(x, np.float32).astype(BF16)


def f64(x):
    return np.asarray(x).astype(np.float64)


E2M1 = np.array([0.0, 0.5, 1.0, 1.5, 2.0, 3.0, 4.0, 6.0, -0.0, -0.5, -1.0, -1.5, -2.0, -3.0, -4.0, -6.0])


def pack_weight(w, fmt):
    k, n = w.shape
    w = f64(bf(w)).reshape(k // 32, 32, n)
    amax = np.abs(w).max(1)
    if fmt == "e4m3":
        byte = np.frexp(amax)[1] - 1 + 127 - 7
    else:
        mant, ex = np.frexp(amax / 6.0)
        byte = np.where(mant > 0.5, ex, ex - 1) + 127
    byte = np.clip(np.where(amax > 0, byte, 1), 1, 254)
    scaled = (w * np.exp2(127.0 - byte)[:, None, :]).reshape(k, n).astype(np.float32)
    by_word = np.ascontiguousarray(scaled.reshape(k // 512, 128, 4, n).transpose(0, 1, 3, 2))
    if fmt == "e4m3":
        words = by_word.astype(ml_dtypes.float8_e4m3fn).view(np.uint8)
    else:
        c = by_word.astype(ml_dtypes.float4_e2m1fn).view(np.uint8) & 0xF
        words = c[..., 0::2] | (c[..., 1::2] << 4)
    return np.ascontiguousarray(words), np.ascontiguousarray(byte.astype(np.uint8).reshape(k // 512, 16, n))


def unpack_weight(words, scales, fmt):
    g, p, n, _ = words.shape
    if fmt == "e4m3":
        vals = np.ascontiguousarray(words).view(ml_dtypes.float8_e4m3fn).astype(np.float64)
    else:
        nib = np.empty((g, p, n, 4), np.uint8)
        nib[..., 0::2] = words & 0xF
        nib[..., 1::2] = words >> 4
        vals = E2M1[nib]
    vals = vals * np.repeat(np.exp2(scales.astype(np.float64) - 127.0), 8, axis=1)[..., None]
    return vals.transpose(0, 1, 3, 2).reshape(g * 512, n)


T, B, I, H = 4, 128, 16384, 128


def sigmoid(v):
    return 1.0 / (1.0 + np.exp(-v))


def setup_inputs():
    s = mx_kscale(I)
    inp = bf(np.random.standard_normal((T, B, I)) * s)
    h0 = bf(np.random.standard_normal((B, H)))
    c0 = bf(np.random.standard_normal((B, H)))
    noise = bf(np.random.standard_normal((B, H)) * 0.3)
    w_ih = np.random.standard_normal((4 * H, I)) / np.sqrt(I) / s[None, :]
    words, scales = pack_weight(np.ascontiguousarray(w_ih.T), "e4m3")
    return {
        "input": inp,
        "h0": h0,
        "c0": c0,
        "noise": noise,
        "W_ih_words": words,
        "W_ih_scales": scales,
        "W_hh": bf(np.random.standard_normal((4 * H, H)) * 0.7 / np.sqrt(H)),
        "b_ih": bf(np.random.standard_normal(4 * H) * 0.3),
        "b_hh": bf(np.random.standard_normal(4 * H) * 0.3),
    }


def reference(input, h0, c0, noise, W_ih_words, W_ih_scales, W_hh, b_ih, b_hh):
    hsz = h0.shape[-1]
    gx = mxq(f64(input), 2, "e4m3") @ unpack_weight(W_ih_words, W_ih_scales, "e4m3")
    gh = f64(h0) @ f64(W_hh).T
    gates = gx + gh[None, :, :] + (f64(b_ih) + f64(b_hh))
    i_g = sigmoid(gates[..., 0 * hsz:1 * hsz])
    f_g = sigmoid(gates[..., 1 * hsz:2 * hsz])
    g_g = np.tanh(gates[..., 2 * hsz:3 * hsz])
    o_g = sigmoid(gates[..., 3 * hsz:4 * hsz])
    c = f_g * f64(c0)[None] + i_g * g_g
    h = o_g * np.tanh(c) + f64(noise)[None]
    return (h, np.stack([h[-1], c[-1]]))

@@ -1,0 +1,248 @@
+from contextlib import ExitStack
+
+import concourse.mybir as mybir
+from concourse.masks import make_identity
+
+F32 = mybir.dt.float32
+BF16 = mybir.dt.bfloat16
+I32 = mybir.dt.int32
+U32 = mybir.dt.uint32
+U8 = mybir.dt.uint8
+FP8X4 = mybir.dt.float8_e4m3fn_x4
+ACT = mybir.ActivationFunctionType
+
+P = 128
+STEPS = 4
+K = 16384
+HIDDEN = 128
+GATE_COLS = 4 * HIDDEN
+PACK = 4
+K_PASS = P * PACK
+BLOCK_PARTS = 8
+BLOCKS = P // BLOCK_PARTS
+PASSES = 8
+CHUNK_K = PASSES * K_PASS
+CHUNKS = K // CHUNK_K
+ROUNDS = CHUNKS * STEPS
+PAIRS = 2
+BANK_PASSES = 2
+HALF_PASSES = PASSES // 2
+RAW_BUFS = 6
+
+FLOPS = 2 * STEPS * P * GATE_COLS * K + 2 * P * GATE_COLS * HIDDEN
+
+
+def tile_lstmlayer_k_kernel(
+    tc, x, h0, c0, noise, w_words, w_scales, w_hh, b_ih, b_hh, out_h, out_state
+):
+    nc = tc.nc
+
+    w_rows = w_words.rearrange("g p n t -> (g p) (n t)").bitcast(I32)
+    w_by_pass = w_rows.rearrange(
+        "(j q s i) w -> j s q i w", j=CHUNKS, q=BLOCKS, s=PASSES, i=BLOCK_PARTS
+    )
+    scale_rows = w_scales.rearrange("g q n -> (g q) n").bitcast(I32)
+    scale_by_quadrant = scale_rows.rearrange(
+        "(j a r s) w -> a j r (s w)", j=CHUNKS, a=4, r=4, s=PASSES
+    )
+
+    with ExitStack() as ctx:
+        const = ctx.enter_context(tc.tile_pool(name="const", bufs=1))
+        raw_pool = ctx.enter_context(tc.tile_pool(name="raw", bufs=RAW_BUFS))
+        sorted_pool = ctx.enter_context(tc.tile_pool(name="sorted", bufs=2))
+        grouped_pool = ctx.enter_context(tc.tile_pool(name="grouped", bufs=2))
+        codes_pool = ctx.enter_context(tc.tile_pool(name="codes", bufs=3))
+        cell_pool = ctx.enter_context(tc.tile_pool(name="cell", bufs=2))
+        acc_pool = ctx.enter_context(tc.psum_pool(name="acc", bufs=1))
+        turn_pool = ctx.enter_context(tc.psum_pool(name="turn", bufs=4))
+        ctx.enter_context(tc.manual_schedule())
+
+        w_planes = const.tile([P, PASSES * GATE_COLS], U8, align_bytes=64)
+        nc.vector.memset(w_planes[:].bitcast(I32), 0)
+        bias_rows = const.tile([P, GATE_COLS], BF16)
+        nc.vector.memset(bias_rows[:], 0.0)
+        ones = const.tile([P, P], BF16)
+        nc.vector.memset(ones[:], 1.0)
+        ident_f32 = const.tile([P, P], F32)
+        make_identity(nc, ident_f32[:])
+        ident_bf16 = const.tile([P, P], BF16)
+        make_identity(nc, ident_bf16[:])
+        table_in = const.tile([P, 1], F32)
+        nc.vector.memset(table_in[:], 0.0)
+        table_out = const.tile([P, 1], F32)
+        nc.scalar.activation(out=table_out[:], in_=table_in[:], func=ACT.Sigmoid)
+
+        w_codes = [
+            const.tile([P, GATE_COLS], U32, name="w_codes%d" % w, align_bytes=64)
+            for w in range(CHUNKS * PASSES)
+        ]
+        acc = [
+            acc_pool.tile([P, GATE_COLS], F32, name="acc%d" % m) for m in range(STEPS)
+        ]
+        raw = {}
+        in_order = {}
+        grouped = {}
+        x_codes = {}
+        x_planes = {}
+
+        def load_x(r):
+            j, m = divmod(r, STEPS)
+            x_raw = raw_pool.tile([P, CHUNK_K], BF16)
+            nc.sync.dma_start(out=x_raw[:], in_=x[m, :, j * CHUNK_K : (j + 1) * CHUNK_K])
+            raw[r] = x_raw
+
+        def load_w_chunk(j):
+            for s in range(PASSES):
+                nc.sync.dma_start(out=w_codes[j * PASSES + s][:].bitcast(I32), in_=w_by_pass[j, s])
+
+        def load_round(r):
+            load_x(r)
+            if r % STEPS == 0:
+                load_w_chunk(r // STEPS)
+
+        def sort_words(r, half):
+            if half == 0:
+                x_sorted = sorted_pool.tile([P, PASSES, PAIRS, P], F32)
+                in_order[r] = x_sorted
+            some = slice(half * HALF_PASSES, (half + 1) * HALF_PASSES)
+            nc.vector.tensor_copy(
+                out=in_order[r][:, some].rearrange("b s u (q i) -> b s u q i", q=BLOCKS),
+                in_=raw[r][:]
+                .bitcast(F32)
+                .rearrange("b (q s i u) -> b s u q i", q=BLOCKS, s=PASSES, i=BLOCK_PARTS)[:, some],
+            )
+            if half == 1 and r + RAW_BUFS < ROUNDS:
+                load_round(r + RAW_BUFS)
+
+        def transpose_round(r):
+            x_grouped = grouped_pool.tile([P, PASSES * K_PASS], BF16, align_bytes=64)
+            grouped[r] = x_grouped
+            grouped_words = x_grouped[:].bitcast(F32).rearrange("p (s b u) -> p s b u", s=PASSES, u=PAIRS)
+            for first in range(0, PASSES, BANK_PASSES):
+                turned = turn_pool.tile([P, BANK_PASSES, PAIRS, P], F32, tag="turned")
+                for s in range(BANK_PASSES):
+                    for u in range(PAIRS):
+                        nc.tensor.transpose(turned[:, s, u, :], in_order[r][:, first + s, u, :], ident_f32[:])
+                nc.scalar.copy(
+                    out=grouped_words[:, first : first + BANK_PASSES],
+                    in_=turned[:].rearrange("p s u b -> p s b u"),
+                )
+
+        def quantise(r, half):
+            if half == 0:
+                codes = codes_pool.tile([P, PASSES * P], U32, align_bytes=64)
+                x_codes[r] = codes
+                plane = codes_pool.tile([P, PASSES * P], U8, align_bytes=64)
+                x_planes[r] = plane
+            cols = slice(half * HALF_PASSES * P, (half + 1) * HALF_PASSES * P)
+            nc.vector.quantize_mx(
+                out=x_codes[r][:, cols].bitcast(FP8X4),
+                scales=x_planes[r][:, cols],
+                in_=grouped[r][:, half * HALF_PASSES * K_PASS : (half + 1) * HALF_PASSES * K_PASS],
+            )
+
+        def multiply(r):
+            j, m = divmod(r, STEPS)
+            for s in range(PASSES):
+                rows = slice(s * P, (s + 1) * P)
+                nc.tensor.matmul_mx(
+                    out=acc[m][:],
+                    lhsT=x_codes[r][:, rows].bitcast(FP8X4),
+                    lhsT_scale=x_planes[r][:, rows],
+                    rhs=w_codes[j * PASSES + s][:].bitcast(FP8X4),
+                    rhs_scale=w_planes[4 * j : P, s * GATE_COLS : (s + 1) * GATE_COLS],
+                    start=(j == 0 and s == 0),
+                    stop=(j == CHUNKS - 1 and s == PASSES - 1),
+                )
+
+        c_new = {}
+        out_gate = {}
+
+        def cell_state(m):
+            gates = cell_pool.tile([P, GATE_COLS], F32)
+            nc.vector.tensor_add(out=gates[:], in0=acc[m][:], in1=base[:])
+            in_forget = cell_pool.tile([P, 2 * HIDDEN], F32)
+            nc.scalar.activation(out=in_forget[:], in_=gates[:, 0 : 2 * HIDDEN], func=ACT.Sigmoid)
+            candidate = cell_pool.tile([P, HIDDEN], F32)
+            nc.scalar.activation(out=candidate[:], in_=gates[:, 2 * HIDDEN : 3 * HIDDEN], func=ACT.Tanh)
+            o_gate = cell_pool.tile([P, HIDDEN], F32)
+            nc.scalar.activation(out=o_gate[:], in_=gates[:, 3 * HIDDEN : 4 * HIDDEN], func=ACT.Sigmoid)
+            out_gate[m] = o_gate
+            kept = cell_pool.tile([P, HIDDEN], F32)
+            nc.vector.tensor_mul(out=kept[:], in0=in_forget[:, HIDDEN : 2 * HIDDEN], in1=c0_sb[:])
+            fresh = cell_pool.tile([P, HIDDEN], F32)
+            nc.vector.tensor_mul(out=fresh[:], in0=in_forget[:, 0:HIDDEN], in1=candidate[:])
+            c_m = cell_pool.tile([P, HIDDEN], F32)
+            nc.vector.tensor_add(out=c_m[:], in0=kept[:], in1=fresh[:])
+            c_new[m] = c_m
+            if m == STEPS - 1:
+                nc.sync.dma_start(out=out_state[1], in_=c_m[:])
+
+        def cell_output(m):
+            tanh_c = cell_pool.tile([P, HIDDEN], F32)
+            nc.scalar.activation(out=tanh_c[:], in_=c_new[m][:], func=ACT.Tanh)
+            gated = cell_pool.tile([P, HIDDEN], F32)
+            nc.vector.tensor_mul(out=gated[:], in0=out_gate[m][:], in1=tanh_c[:])
+            h_m = cell_pool.tile([P, HIDDEN], F32)
+            nc.vector.tensor_add(out=h_m[:], in0=gated[:], in1=noise_sb[:])
+            nc.sync.dma_start(out=out_h[m], in_=h_m[:])
+            if m == STEPS - 1:
+                nc.sync.dma_start(out=out_state[0], in_=h_m[:])
+
+        load_x(0)
+        plain_in = const.tile([P, 1 + 4, HIDDEN], BF16)
+        nc.sync.dma_start(out=plain_in[:, 0, :], in_=h0)
+        nc.sync.dma_start(out=plain_in[:, 1:5, :], in_=w_hh.rearrange("(a n) h -> n a h", n=P))
+        nc.sync.dma_start(out=bias_rows[0:1, :], in_=b_ih.unsqueeze(0))
+        nc.sync.dma_start(out=bias_rows[1:2, :], in_=b_hh.unsqueeze(0))
+        for a in range(4):
+            nc.sync.dma_start(out=w_planes[32 * a : 32 * a + 16, :].bitcast(I32), in_=scale_by_quadrant[a])
+        load_w_chunk(0)
+        for r in range(1, RAW_BUFS):
+            load_round(r)
+        c0_sb = const.tile([P, HIDDEN], BF16)
+        nc.sync.dma_start(out=c0_sb[:], in_=c0)
+        noise_sb = const.tile([P, HIDDEN], BF16)
+        nc.sync.dma_start(out=noise_sb[:], in_=noise)
+
+        sort_words(0, 0)
+        sort_words(0, 1)
+        transpose_round(0)
+
+        plain_turned = turn_pool.tile([P, 1 + 4, P], BF16, tag="turned")
+        for a in range(1 + 4):
+            nc.tensor.transpose(plain_turned[:, a, :], plain_in[:, a, :], ident_bf16[:])
+        plain_t = const.tile([P, 1 + 4, P], BF16)
+        nc.vector.tensor_copy(out=plain_t[:], in_=plain_turned[:])
+        base_sum = turn_pool.tile([P, GATE_COLS], F32, tag="turned")
+        nc.tensor.matmul(
+            out=base_sum[:],
+            lhsT=plain_t[:, 0, :],
+            rhs=plain_t[:, 1:5, :].rearrange("h a n -> h (a n)"),
+            start=True,
+            stop=False,
+        )
+        nc.tensor.matmul(out=base_sum[:], lhsT=ones[:], rhs=bias_rows[:], start=False, stop=True)
+        base = const.tile([P, GATE_COLS], F32)
+        nc.vector.tensor_copy(out=base[:], in_=base_sum[:])
+
+        quantise(0, 0)
+        quantise(0, 1)
+        sort_words(1, 0)
+        sort_words(1, 1)
+
+        for r in range(ROUNDS):
+            if r + 1 < ROUNDS:
+                transpose_round(r + 1)
+            for half in range(2):
+                if r + 1 < ROUNDS:
+                    quantise(r + 1, half)
+                if r + 2 < ROUNDS:
+                    sort_words(r + 2, half)
+            done = r - (ROUNDS - STEPS)
+            if done >= 1:
+                cell_output(done - 1)
+            multiply(r)
+            if done >= 0:
+                cell_state(done)
+        cell_output(STEPS - 1)

@@ -26,7 +26,8 @@ CHUNKS = K // CHUNK_K
 ROUNDS = CHUNKS * STEPS
 PAIRS = 2
 BANK_PASSES = 2
-HALF_PASSES = PASSES // 2
+UNIT_PASSES = PASSES // 2
+UNITS = ROUNDS * PASSES // UNIT_PASSES
 RAW_BUFS = 6
 
 FLOPS = 2 * STEPS * P * GATE_COLS * K + 2 * P * GATE_COLS * HIDDEN
@@ -49,8 +50,8 @@ def tile_lstmlayer_k_kernel(
     with ExitStack() as ctx:
         const = ctx.enter_context(tc.tile_pool(name="const", bufs=1))
         raw_pool = ctx.enter_context(tc.tile_pool(name="raw", bufs=RAW_BUFS))
-        sorted_pool = ctx.enter_context(tc.tile_pool(name="sorted", bufs=2))
-        grouped_pool = ctx.enter_context(tc.tile_pool(name="grouped", bufs=2))
+        sorted_pool = ctx.enter_context(tc.tile_pool(name="sorted", bufs=3))
+        grouped_pool = ctx.enter_context(tc.tile_pool(name="grouped", bufs=3))
         codes_pool = ctx.enter_context(tc.tile_pool(name="codes", bufs=3))
         cell_pool = ctx.enter_context(tc.tile_pool(name="cell", bufs=2))
         acc_pool = ctx.enter_context(tc.psum_pool(name="acc", bufs=1))
@@ -100,13 +101,13 @@ def tile_lstmlayer_k_kernel(
             if r % STEPS == 0:
                 load_w_chunk(r // STEPS)
 
-        def sort_words(r, half):
-            if half == 0:
-                x_sorted = sorted_pool.tile([P, PASSES, PAIRS, P], F32)
-                in_order[r] = x_sorted
-            some = slice(half * HALF_PASSES, (half + 1) * HALF_PASSES)
+        def sort_words(v):
+            r, half = divmod(v, 2)
+            some = slice(half * UNIT_PASSES, (half + 1) * UNIT_PASSES)
+            x_sorted = sorted_pool.tile([P, UNIT_PASSES, PAIRS, P], F32)
+            in_order[v] = x_sorted
             nc.vector.tensor_copy(
-                out=in_order[r][:, some].rearrange("b s u (q i) -> b s u q i", q=BLOCKS),
+                out=x_sorted[:].rearrange("b s u (q i) -> b s u q i", q=BLOCKS),
                 in_=raw[r][:]
                 .bitcast(F32)
                 .rearrange("b (q s i u) -> b s u q i", q=BLOCKS, s=PASSES, i=BLOCK_PARTS)[:, some],
@@ -114,41 +115,37 @@ def tile_lstmlayer_k_kernel(
             if half == 1 and r + RAW_BUFS < ROUNDS:
                 load_round(r + RAW_BUFS)
 
-        def transpose_round(r):
-            x_grouped = grouped_pool.tile([P, PASSES * K_PASS], BF16, align_bytes=64)
-            grouped[r] = x_grouped
-            grouped_words = x_grouped[:].bitcast(F32).rearrange("p (s b u) -> p s b u", s=PASSES, u=PAIRS)
-            for first in range(0, PASSES, BANK_PASSES):
+        def transpose_unit(v):
+            x_grouped = grouped_pool.tile([P, UNIT_PASSES * K_PASS], BF16, align_bytes=64)
+            grouped[v] = x_grouped
+            grouped_words = x_grouped[:].bitcast(F32).rearrange("p (s b u) -> p s b u", s=UNIT_PASSES, u=PAIRS)
+            for first in range(0, UNIT_PASSES, BANK_PASSES):
                 turned = turn_pool.tile([P, BANK_PASSES, PAIRS, P], F32, tag="turned")
                 for s in range(BANK_PASSES):
                     for u in range(PAIRS):
-                        nc.tensor.transpose(turned[:, s, u, :], in_order[r][:, first + s, u, :], ident_f32[:])
+                        nc.tensor.transpose(turned[:, s, u, :], in_order[v][:, first + s, u, :], ident_f32[:])
                 nc.scalar.copy(
                     out=grouped_words[:, first : first + BANK_PASSES],
                     in_=turned[:].rearrange("p s u b -> p s b u"),
                 )
 
-        def quantise(r, half):
-            if half == 0:
-                codes = codes_pool.tile([P, PASSES * P], U32, align_bytes=64)
-                x_codes[r] = codes
-                plane = codes_pool.tile([P, PASSES * P], U8, align_bytes=64)
-                x_planes[r] = plane
-            cols = slice(half * HALF_PASSES * P, (half + 1) * HALF_PASSES * P)
-            nc.vector.quantize_mx(
-                out=x_codes[r][:, cols].bitcast(FP8X4),
-                scales=x_planes[r][:, cols],
-                in_=grouped[r][:, half * HALF_PASSES * K_PASS : (half + 1) * HALF_PASSES * K_PASS],
-            )
+        def quantise(v):
+            codes = codes_pool.tile([P, UNIT_PASSES * P], U32, align_bytes=64)
+            x_codes[v] = codes
+            plane = codes_pool.tile([P, UNIT_PASSES * P], U8, align_bytes=64)
+            x_planes[v] = plane
+            nc.vector.quantize_mx(out=codes[:].bitcast(FP8X4), scales=plane[:], in_=grouped[v][:])
 
-        def multiply(r):
+        def multiply(v):
+            r, half = divmod(v, 2)
             j, m = divmod(r, STEPS)
-            for s in range(PASSES):
-                rows = slice(s * P, (s + 1) * P)
+            for n in range(UNIT_PASSES):
+                s = half * UNIT_PASSES + n
+                rows = slice(n * P, (n + 1) * P)
                 nc.tensor.matmul_mx(
                     out=acc[m][:],
-                    lhsT=x_codes[r][:, rows].bitcast(FP8X4),
-                    lhsT_scale=x_planes[r][:, rows],
+                    lhsT=x_codes[v][:, rows].bitcast(FP8X4),
+                    lhsT_scale=x_planes[v][:, rows],
                     rhs=w_codes[j * PASSES + s][:].bitcast(FP8X4),
                     rhs_scale=w_planes[4 * j : P, s * GATE_COLS : (s + 1) * GATE_COLS],
                     start=(j == 0 and s == 0),
@@ -205,9 +202,9 @@ def tile_lstmlayer_k_kernel(
         noise_sb = const.tile([P, HIDDEN], BF16)
         nc.sync.dma_start(out=noise_sb[:], in_=noise)
 
-        sort_words(0, 0)
-        sort_words(0, 1)
-        transpose_round(0)
+        for v in range(2):
+            sort_words(v)
+            transpose_unit(v)
 
         plain_turned = turn_pool.tile([P, 1 + 4, P], BF16, tag="turned")
         for a in range(1 + 4):
@@ -226,23 +223,22 @@ def tile_lstmlayer_k_kernel(
         base = const.tile([P, GATE_COLS], F32)
         nc.vector.tensor_copy(out=base[:], in_=base_sum[:])
 
-        quantise(0, 0)
-        quantise(0, 1)
-        sort_words(1, 0)
-        sort_words(1, 1)
+        quantise(0)
+        sort_words(2)
+        sort_words(3)
 
-        for r in range(ROUNDS):
-            if r + 1 < ROUNDS:
-                transpose_round(r + 1)
-            for half in range(2):
-                if r + 1 < ROUNDS:
-                    quantise(r + 1, half)
-                if r + 2 < ROUNDS:
-                    sort_words(r + 2, half)
-            done = r - (ROUNDS - STEPS)
-            if done >= 1:
+        for v in range(UNITS):
+            if v + 2 < UNITS:
+                transpose_unit(v + 2)
+            if v + 1 < UNITS:
+                quantise(v + 1)
+            if v + 4 < UNITS:
+                sort_words(v + 4)
+            done, odd = divmod(v - 2 * (ROUNDS - STEPS), 2)
+            if done >= 1 and not odd:
+                cell_state(done - 1)
+            if done >= 1 and odd:
                 cell_output(done - 1)
-            multiply(r)
-            if done >= 0:
-                cell_state(done)
+            multiply(v)
+        cell_state(STEPS - 1)
         cell_output(STEPS - 1)

@@ -26,6 +26,7 @@ CHUNKS = K // CHUNK_K
 ROUNDS = CHUNKS * STEPS
 PAIRS = 2
 BANK_PASSES = 2
+LOAD_PASSES = 4
 UNIT_PASSES = PASSES // 2
 UNITS = ROUNDS * PASSES // UNIT_PASSES
 RAW_BUFS = 6
@@ -39,13 +40,9 @@ def tile_lstmlayer_k_kernel(
     nc = tc.nc
 
     w_rows = w_words.rearrange("g p n t -> (g p) (n t)").bitcast(I32)
-    w_by_pass = w_rows.rearrange(
-        "(j q s i) w -> j s q i w", j=CHUNKS, q=BLOCKS, s=PASSES, i=BLOCK_PARTS
-    )
+    w_by_load = w_rows.rearrange("(l s p) w -> l p s w", s=LOAD_PASSES, p=P)
     scale_rows = w_scales.rearrange("g q n -> (g q) n").bitcast(I32)
-    scale_by_quadrant = scale_rows.rearrange(
-        "(j a r s) w -> a j r (s w)", j=CHUNKS, a=4, r=4, s=PASSES
-    )
+    scale_by_quadrant = scale_rows.rearrange("(j s a r) w -> j a r s w", s=PASSES, a=4, r=4)
 
     with ExitStack() as ctx:
         const = ctx.enter_context(tc.tile_pool(name="const", bufs=1))
@@ -74,8 +71,8 @@ def tile_lstmlayer_k_kernel(
         nc.scalar.activation(out=table_out[:], in_=table_in[:], func=ACT.Sigmoid)
 
         w_codes = [
-            const.tile([P, GATE_COLS], U32, name="w_codes%d" % w, align_bytes=64)
-            for w in range(CHUNKS * PASSES)
+            const.tile([P, LOAD_PASSES, GATE_COLS], U32, name="w_codes%d" % l, align_bytes=64)
+            for l in range(CHUNKS * PASSES // LOAD_PASSES)
         ]
         acc = [
             acc_pool.tile([P, GATE_COLS], F32, name="acc%d" % m) for m in range(STEPS)
@@ -93,10 +90,21 @@ def tile_lstmlayer_k_kernel(
             raw[r] = x_raw
 
         def load_w_chunk(j):
-            for s in range(PASSES):
-                nc.sync.dma_start(out=w_codes[j * PASSES + s][:].bitcast(I32), in_=w_by_pass[j, s])
+            for l in range(j * PASSES // LOAD_PASSES, (j + 1) * PASSES // LOAD_PASSES):
+                nc.sync.dma_start(out=w_codes[l][:].bitcast(I32), in_=w_by_load[l])
+
+        def load_scales(j):
+            for a in range(4):
+                nc.sync.dma_start(
+                    out=w_planes[32 * a + 4 * j : 32 * a + 4 * j + 4, :]
+                    .bitcast(I32)
+                    .rearrange("r (s w) -> r s w", s=PASSES),
+                    in_=scale_by_quadrant[j, a],
+                )
 
         def load_round(r):
+            if r % STEPS == 0:
+                load_scales(r // STEPS)
             load_x(r)
             if r % STEPS == 0:
                 load_w_chunk(r // STEPS)
@@ -107,10 +115,10 @@ def tile_lstmlayer_k_kernel(
             x_sorted = sorted_pool.tile([P, UNIT_PASSES, PAIRS, P], F32)
             in_order[v] = x_sorted
             nc.vector.tensor_copy(
-                out=x_sorted[:].rearrange("b s u (q i) -> b s u q i", q=BLOCKS),
+                out=x_sorted[:],
                 in_=raw[r][:]
                 .bitcast(F32)
-                .rearrange("b (q s i u) -> b s u q i", q=BLOCKS, s=PASSES, i=BLOCK_PARTS)[:, some],
+                .rearrange("b (s p u) -> b s u p", s=PASSES, p=P)[:, some],
             )
             if half == 1 and r + RAW_BUFS < ROUNDS:
                 load_round(r + RAW_BUFS)
@@ -146,7 +154,7 @@ def tile_lstmlayer_k_kernel(
                     out=acc[m][:],
                     lhsT=x_codes[v][:, rows].bitcast(FP8X4),
                     lhsT_scale=x_planes[v][:, rows],
-                    rhs=w_codes[j * PASSES + s][:].bitcast(FP8X4),
+                    rhs=w_codes[(j * PASSES + s) // LOAD_PASSES][:, s % LOAD_PASSES, :].bitcast(FP8X4),
                     rhs_scale=w_planes[4 * j : P, s * GATE_COLS : (s + 1) * GATE_COLS],
                     start=(j == 0 and s == 0),
                     stop=(j == CHUNKS - 1 and s == PASSES - 1),
@@ -192,8 +200,7 @@ def tile_lstmlayer_k_kernel(
         nc.sync.dma_start(out=plain_in[:, 1:5, :], in_=w_hh.rearrange("(a n) h -> n a h", n=P))
         nc.sync.dma_start(out=bias_rows[0:1, :], in_=b_ih.unsqueeze(0))
         nc.sync.dma_start(out=bias_rows[1:2, :], in_=b_hh.unsqueeze(0))
-        for a in range(4):
-            nc.sync.dma_start(out=w_planes[32 * a : 32 * a + 16, :].bitcast(I32), in_=scale_by_quadrant[a])
+        load_scales(0)
         load_w_chunk(0)
         for r in range(1, RAW_BUFS):
             load_round(r)

@@ -18,18 +18,19 @@ HIDDEN = 128
 GATE_COLS = 4 * HIDDEN
 PACK = 4
 K_PASS = P * PACK
-BLOCK_PARTS = 8
-BLOCKS = P // BLOCK_PARTS
-PASSES = 8
-CHUNK_K = PASSES * K_PASS
-CHUNKS = K // CHUNK_K
-ROUNDS = CHUNKS * STEPS
 PAIRS = 2
 BANK_PASSES = 2
-LOAD_PASSES = 4
-UNIT_PASSES = PASSES // 2
-UNITS = ROUNDS * PASSES // UNIT_PASSES
-RAW_BUFS = 6
+PASSES = 4
+GROUP_K = PASSES * K_PASS
+GROUPS = K // GROUP_K
+PLANE_PASSES = 8
+SPANS = [(0,), (1,), (2, 3), (4, 5), (6, 7)]
+SPAN_GROUPS = max(len(span) for span in SPANS)
+LOADS = [(span, m) for span in SPANS for m in range(STEPS)]
+UNITS = [(g, m) for span, m in LOADS for g in span]
+RAW_BUFS = 8
+RUN = 2
+BASE_UNIT = 7
 
 FLOPS = 2 * STEPS * P * GATE_COLS * K + 2 * P * GATE_COLS * HIDDEN
 
@@ -39,15 +40,14 @@ def tile_lstmlayer_k_kernel(
 ):
     nc = tc.nc
 
-    w_rows = w_words.rearrange("g p n t -> (g p) (n t)").bitcast(I32)
-    w_by_load = w_rows.rearrange("(l s p) w -> l p s w", s=LOAD_PASSES, p=P)
+    w_rows = w_words.rearrange("g p n t -> g p (n t)").bitcast(I32)
     scale_rows = w_scales.rearrange("g q n -> (g q) n").bitcast(I32)
-    scale_by_quadrant = scale_rows.rearrange("(j s a r) w -> j a r s w", s=PASSES, a=4, r=4)
+    scale_by_quadrant = scale_rows.rearrange("(j s a r) w -> j a r s w", s=PLANE_PASSES, a=4, r=4)
 
     with ExitStack() as ctx:
         const = ctx.enter_context(tc.tile_pool(name="const", bufs=1))
         raw_pool = ctx.enter_context(tc.tile_pool(name="raw", bufs=RAW_BUFS))
-        sorted_pool = ctx.enter_context(tc.tile_pool(name="sorted", bufs=3))
+        sorted_pool = ctx.enter_context(tc.tile_pool(name="sorted", bufs=4))
         grouped_pool = ctx.enter_context(tc.tile_pool(name="grouped", bufs=3))
         codes_pool = ctx.enter_context(tc.tile_pool(name="codes", bufs=3))
         cell_pool = ctx.enter_context(tc.tile_pool(name="cell", bufs=2))
@@ -55,79 +55,104 @@ def tile_lstmlayer_k_kernel(
         turn_pool = ctx.enter_context(tc.psum_pool(name="turn", bufs=4))
         ctx.enter_context(tc.manual_schedule())
 
-        w_planes = const.tile([P, PASSES * GATE_COLS], U8, align_bytes=64)
-        nc.vector.memset(w_planes[:].bitcast(I32), 0)
-        bias_rows = const.tile([P, GATE_COLS], BF16)
-        nc.vector.memset(bias_rows[:], 0.0)
-        ones = const.tile([P, P], BF16)
-        nc.vector.memset(ones[:], 1.0)
+        w_planes = [
+            const.tile([P, PLANE_PASSES * GATE_COLS], U8, name="w_planes%d" % j, align_bytes=64)
+            for j in range(GROUPS * PASSES // PLANE_PASSES)
+        ]
+        nc.vector.memset(w_planes[0][:].bitcast(I32), 0)
         ident_f32 = const.tile([P, P], F32)
         make_identity(nc, ident_f32[:])
+        for plane in w_planes[1:]:
+            nc.gpsimd.memset(plane[:].bitcast(I32), 0)
         ident_bf16 = const.tile([P, P], BF16)
         make_identity(nc, ident_bf16[:])
+        bias_rows = const.tile([P, GATE_COLS], BF16)
+        nc.gpsimd.memset(bias_rows[:], 0.0)
+        ones = const.tile([P, P], BF16)
+        nc.gpsimd.memset(ones[:], 1.0)
         table_in = const.tile([P, 1], F32)
         nc.vector.memset(table_in[:], 0.0)
         table_out = const.tile([P, 1], F32)
         nc.scalar.activation(out=table_out[:], in_=table_in[:], func=ACT.Sigmoid)
 
         w_codes = [
-            const.tile([P, LOAD_PASSES, GATE_COLS], U32, name="w_codes%d" % l, align_bytes=64)
-            for l in range(CHUNKS * PASSES // LOAD_PASSES)
+            const.tile([P, PASSES, GATE_COLS], U32, name="w_codes%d" % g, align_bytes=64)
+            for g in range(GROUPS)
         ]
         acc = [
             acc_pool.tile([P, GATE_COLS], F32, name="acc%d" % m) for m in range(STEPS)
         ]
+        base = const.tile([P, GATE_COLS], F32)
+        plain_in = const.tile([P, 1 + 4, HIDDEN], BF16)
+        plain_t = const.tile([P, 1 + 4, P], BF16)
+        c0_sb = const.tile([P, HIDDEN], BF16)
+        noise_sb = const.tile([P, HIDDEN], BF16)
         raw = {}
         in_order = {}
         grouped = {}
         x_codes = {}
         x_planes = {}
 
-        def load_x(r):
-            j, m = divmod(r, STEPS)
-            x_raw = raw_pool.tile([P, CHUNK_K], BF16)
-            nc.sync.dma_start(out=x_raw[:], in_=x[m, :, j * CHUNK_K : (j + 1) * CHUNK_K])
-            raw[r] = x_raw
-
-        def load_w_chunk(j):
-            for l in range(j * PASSES // LOAD_PASSES, (j + 1) * PASSES // LOAD_PASSES):
-                nc.sync.dma_start(out=w_codes[l][:].bitcast(I32), in_=w_by_load[l])
+        def load_w(g, passes):
+            for first in range(0, PASSES, passes):
+                some = slice(PASSES * g + first, PASSES * g + first + passes)
+                nc.sync.dma_start(
+                    out=w_codes[g][:, first : first + passes, :].bitcast(I32),
+                    in_=w_rows[some].rearrange("s p w -> p s w"),
+                )
 
         def load_scales(j):
             for a in range(4):
                 nc.sync.dma_start(
-                    out=w_planes[32 * a + 4 * j : 32 * a + 4 * j + 4, :]
+                    out=w_planes[j][32 * a + 4 * j : 32 * a + 4 * j + 4, :]
                     .bitcast(I32)
-                    .rearrange("r (s w) -> r s w", s=PASSES),
+                    .rearrange("r (s w) -> r s w", s=PLANE_PASSES),
                     in_=scale_by_quadrant[j, a],
                 )
 
-        def load_round(r):
-            if r % STEPS == 0:
-                load_scales(r // STEPS)
-            load_x(r)
-            if r % STEPS == 0:
-                load_w_chunk(r // STEPS)
+        def load_plain():
+            nc.sync.dma_start(out=plain_in[:, 0, :], in_=h0)
+            nc.sync.dma_start(out=plain_in[:, 1:5, :], in_=w_hh.rearrange("(a n) h -> n a h", n=P))
+            nc.sync.dma_start(out=bias_rows[0:1, :], in_=b_ih.unsqueeze(0))
+            nc.sync.dma_start(out=bias_rows[1:2, :], in_=b_hh.unsqueeze(0))
+            nc.sync.dma_start(out=c0_sb[:], in_=c0)
+            nc.sync.dma_start(out=noise_sb[:], in_=noise)
+
+        def load(n):
+            span, m = LOADS[n]
+            x_raw = raw_pool.tile([P, SPAN_GROUPS * GROUP_K], BF16)
+            width = len(span) * GROUP_K
+            nc.sync.dma_start(
+                out=x_raw[:, :width], in_=x[m, :, span[0] * GROUP_K : span[0] * GROUP_K + width]
+            )
+            for g in span:
+                raw[g, m] = x_raw[:, (g - span[0]) * GROUP_K : (g - span[0] + 1) * GROUP_K]
+            if m == {0: 2, 1: 3}.get(span[0], 1):
+                for g in span:
+                    if g % 2 == 0:
+                        load_scales(g // 2)
+                    load_w(g, 2 if g == 0 else PASSES)
+            if n == STEPS:
+                load_plain()
 
         def sort_words(v):
-            r, half = divmod(v, 2)
-            some = slice(half * UNIT_PASSES, (half + 1) * UNIT_PASSES)
-            x_sorted = sorted_pool.tile([P, UNIT_PASSES, PAIRS, P], F32)
+            g, m = UNITS[v]
+            x_sorted = sorted_pool.tile([P, PASSES, PAIRS, P], F32)
             in_order[v] = x_sorted
             nc.vector.tensor_copy(
                 out=x_sorted[:],
-                in_=raw[r][:]
-                .bitcast(F32)
-                .rearrange("b (s p u) -> b s u p", s=PASSES, p=P)[:, some],
+                in_=raw[g, m].bitcast(F32).rearrange("b (s p u) -> b s u p", s=PASSES, p=P),
             )
-            if half == 1 and r + RAW_BUFS < ROUNDS:
-                load_round(r + RAW_BUFS)
+            done = [n for n in range(len(LOADS)) if LOADS[n][1] == m and LOADS[n][0][-1] == g]
+            for n in done:
+                if n + RAW_BUFS < len(LOADS):
+                    load(n + RAW_BUFS)
 
         def transpose_unit(v):
-            x_grouped = grouped_pool.tile([P, UNIT_PASSES * K_PASS], BF16, align_bytes=64)
+            x_grouped = grouped_pool.tile([P, PASSES * K_PASS], BF16, align_bytes=64)
             grouped[v] = x_grouped
-            grouped_words = x_grouped[:].bitcast(F32).rearrange("p (s b u) -> p s b u", s=UNIT_PASSES, u=PAIRS)
-            for first in range(0, UNIT_PASSES, BANK_PASSES):
+            grouped_words = x_grouped[:].bitcast(F32).rearrange("p (s b u) -> p s b u", s=PASSES, u=PAIRS)
+            for first in range(0, PASSES, BANK_PASSES):
                 turned = turn_pool.tile([P, BANK_PASSES, PAIRS, P], F32, tag="turned")
                 for s in range(BANK_PASSES):
                     for u in range(PAIRS):
@@ -138,34 +163,51 @@ def tile_lstmlayer_k_kernel(
                 )
 
         def quantise(v):
-            codes = codes_pool.tile([P, UNIT_PASSES * P], U32, align_bytes=64)
+            codes = codes_pool.tile([P, PASSES * P], U32, align_bytes=64)
             x_codes[v] = codes
-            plane = codes_pool.tile([P, UNIT_PASSES * P], U8, align_bytes=64)
+            plane = codes_pool.tile([P, PASSES * P], U8, align_bytes=64)
             x_planes[v] = plane
             nc.vector.quantize_mx(out=codes[:].bitcast(FP8X4), scales=plane[:], in_=grouped[v][:])
 
         def multiply(v):
-            r, half = divmod(v, 2)
-            j, m = divmod(r, STEPS)
-            for n in range(UNIT_PASSES):
-                s = half * UNIT_PASSES + n
-                rows = slice(n * P, (n + 1) * P)
+            g, m = UNITS[v]
+            for s in range(PASSES):
+                rows = slice(s * P, (s + 1) * P)
+                j, slot = divmod(g * PASSES + s, PLANE_PASSES)
                 nc.tensor.matmul_mx(
                     out=acc[m][:],
                     lhsT=x_codes[v][:, rows].bitcast(FP8X4),
                     lhsT_scale=x_planes[v][:, rows],
-                    rhs=w_codes[(j * PASSES + s) // LOAD_PASSES][:, s % LOAD_PASSES, :].bitcast(FP8X4),
-                    rhs_scale=w_planes[4 * j : P, s * GATE_COLS : (s + 1) * GATE_COLS],
-                    start=(j == 0 and s == 0),
-                    stop=(j == CHUNKS - 1 and s == PASSES - 1),
+                    rhs=w_codes[g][:, s, :].bitcast(FP8X4),
+                    rhs_scale=w_planes[j][4 * j : P, slot * GATE_COLS : (slot + 1) * GATE_COLS],
+                    start=(g == 0 and s == 0),
+                    stop=(g == GROUPS - 1 and s == PASSES - 1),
                 )
+
+        def compute_base():
+            plain_turned = turn_pool.tile([P, 1 + 4, P], BF16, tag="turned")
+            for a in range(1 + 4):
+                nc.tensor.transpose(plain_turned[:, a, :], plain_in[:, a, :], ident_bf16[:])
+            nc.vector.tensor_copy(out=plain_t[:], in_=plain_turned[:])
+            base_sum = turn_pool.tile([P, GATE_COLS], F32, tag="turned")
+            nc.tensor.matmul(
+                out=base_sum[:],
+                lhsT=plain_t[:, 0, :],
+                rhs=plain_t[:, 1:5, :].rearrange("h a n -> h (a n)"),
+                start=True,
+                stop=False,
+            )
+            nc.tensor.matmul(out=base_sum[:], lhsT=ones[:], rhs=bias_rows[:], start=False, stop=True)
+            nc.vector.tensor_copy(out=base[:], in_=base_sum[:])
 
         c_new = {}
         out_gate = {}
 
         def cell_state(m):
             gates = cell_pool.tile([P, GATE_COLS], F32)
-            nc.vector.tensor_add(out=gates[:], in0=acc[m][:], in1=base[:])
+            for first in (0, 2 * HIDDEN):
+                cols = slice(first, first + 2 * HIDDEN)
+                nc.vector.tensor_add(out=gates[:, cols], in0=acc[m][:, cols], in1=base[:, cols])
             in_forget = cell_pool.tile([P, 2 * HIDDEN], F32)
             nc.scalar.activation(out=in_forget[:], in_=gates[:, 0 : 2 * HIDDEN], func=ACT.Sigmoid)
             candidate = cell_pool.tile([P, HIDDEN], F32)
@@ -194,58 +236,44 @@ def tile_lstmlayer_k_kernel(
             if m == STEPS - 1:
                 nc.sync.dma_start(out=out_state[0], in_=h_m[:])
 
-        load_x(0)
-        plain_in = const.tile([P, 1 + 4, HIDDEN], BF16)
-        nc.sync.dma_start(out=plain_in[:, 0, :], in_=h0)
-        nc.sync.dma_start(out=plain_in[:, 1:5, :], in_=w_hh.rearrange("(a n) h -> n a h", n=P))
-        nc.sync.dma_start(out=bias_rows[0:1, :], in_=b_ih.unsqueeze(0))
-        nc.sync.dma_start(out=bias_rows[1:2, :], in_=b_hh.unsqueeze(0))
-        load_scales(0)
-        load_w_chunk(0)
-        for r in range(1, RAW_BUFS):
-            load_round(r)
-        c0_sb = const.tile([P, HIDDEN], BF16)
-        nc.sync.dma_start(out=c0_sb[:], in_=c0)
-        noise_sb = const.tile([P, HIDDEN], BF16)
-        nc.sync.dma_start(out=noise_sb[:], in_=noise)
-
-        for v in range(2):
+        for n in range(RAW_BUFS):
+            load(n)
+        for v in range(3):
             sort_words(v)
             transpose_unit(v)
-
-        plain_turned = turn_pool.tile([P, 1 + 4, P], BF16, tag="turned")
-        for a in range(1 + 4):
-            nc.tensor.transpose(plain_turned[:, a, :], plain_in[:, a, :], ident_bf16[:])
-        plain_t = const.tile([P, 1 + 4, P], BF16)
-        nc.vector.tensor_copy(out=plain_t[:], in_=plain_turned[:])
-        base_sum = turn_pool.tile([P, GATE_COLS], F32, tag="turned")
-        nc.tensor.matmul(
-            out=base_sum[:],
-            lhsT=plain_t[:, 0, :],
-            rhs=plain_t[:, 1:5, :].rearrange("h a n -> h (a n)"),
-            start=True,
-            stop=False,
-        )
-        nc.tensor.matmul(out=base_sum[:], lhsT=ones[:], rhs=bias_rows[:], start=False, stop=True)
-        base = const.tile([P, GATE_COLS], F32)
-        nc.vector.tensor_copy(out=base[:], in_=base_sum[:])
-
         quantise(0)
-        sort_words(2)
         sort_words(3)
+        quantise(1)
+        multiply(0)
+        transpose_unit(3)
+        sort_words(4)
+        quantise(2)
+        sort_words(5)
+        multiply(1)
 
-        for v in range(UNITS):
-            if v + 2 < UNITS:
+        count = len(UNITS)
+        finished = None
+        for v in range(RUN, count, RUN):
+            if v + 2 < count:
                 transpose_unit(v + 2)
-            if v + 1 < UNITS:
-                quantise(v + 1)
-            if v + 4 < UNITS:
+            quantise(v + 1)
+            if finished is not None:
+                cell_state(finished)
+            if v + 3 < count:
+                transpose_unit(v + 3)
+            if v + 4 < count:
                 sort_words(v + 4)
-            done, odd = divmod(v - 2 * (ROUNDS - STEPS), 2)
-            if done >= 1 and not odd:
-                cell_state(done - 1)
-            if done >= 1 and odd:
-                cell_output(done - 1)
+            if v + 2 < count:
+                quantise(v + 2)
+            if v + 5 < count:
+                sort_words(v + 5)
+            if finished is not None:
+                cell_output(finished)
             multiply(v)
-        cell_state(STEPS - 1)
-        cell_output(STEPS - 1)
+            multiply(v + 1)
+            g, m = UNITS[v + 1]
+            finished = m if g == GROUPS - 1 else None
+            if v + 1 == BASE_UNIT:
+                compute_base()
+        cell_state(finished)
+        cell_output(finished)

@@ -24,13 +24,14 @@ PASSES = 4
 GROUP_K = PASSES * K_PASS
 GROUPS = K // GROUP_K
 PLANE_PASSES = 8
-SPANS = [(0,), (1,), (2, 3), (4, 5), (6, 7)]
+SPANS = [(0,), (1,), (2,), (3,), (4,), (5,), (6, 7)]
 SPAN_GROUPS = max(len(span) for span in SPANS)
 LOADS = [(span, m) for span in SPANS for m in range(STEPS)]
 UNITS = [(g, m) for span, m in LOADS for g in span]
 RAW_BUFS = 8
 RUN = 2
-BASE_UNIT = 7
+PLAIN_LOAD = 20
+BASE_UNIT = 23
 
 FLOPS = 2 * STEPS * P * GATE_COLS * K + 2 * P * GATE_COLS * HIDDEN
 
@@ -42,14 +43,14 @@ def tile_lstmlayer_k_kernel(
 
     w_rows = w_words.rearrange("g p n t -> g p (n t)").bitcast(I32)
     scale_rows = w_scales.rearrange("g q n -> (g q) n").bitcast(I32)
-    scale_by_quadrant = scale_rows.rearrange("(j s a r) w -> j a r s w", s=PLANE_PASSES, a=4, r=4)
+    scale_by_place = scale_rows.rearrange("(j s a r) w -> j r a s w", s=PLANE_PASSES, a=4, r=4)
 
     with ExitStack() as ctx:
         const = ctx.enter_context(tc.tile_pool(name="const", bufs=1))
         raw_pool = ctx.enter_context(tc.tile_pool(name="raw", bufs=RAW_BUFS))
         sorted_pool = ctx.enter_context(tc.tile_pool(name="sorted", bufs=4))
         grouped_pool = ctx.enter_context(tc.tile_pool(name="grouped", bufs=3))
-        codes_pool = ctx.enter_context(tc.tile_pool(name="codes", bufs=3))
+        codes_pool = ctx.enter_context(tc.tile_pool(name="codes", bufs=4))
         cell_pool = ctx.enter_context(tc.tile_pool(name="cell", bufs=2))
         acc_pool = ctx.enter_context(tc.psum_pool(name="acc", bufs=1))
         turn_pool = ctx.enter_context(tc.psum_pool(name="turn", bufs=4))
@@ -102,12 +103,12 @@ def tile_lstmlayer_k_kernel(
                 )
 
         def load_scales(j):
-            for a in range(4):
+            for r in range(4):
                 nc.sync.dma_start(
-                    out=w_planes[j][32 * a + 4 * j : 32 * a + 4 * j + 4, :]
+                    out=w_planes[j][4 * j + r : P : 32, :]
                     .bitcast(I32)
-                    .rearrange("r (s w) -> r s w", s=PLANE_PASSES),
-                    in_=scale_by_quadrant[j, a],
+                    .rearrange("a (s w) -> a s w", s=PLANE_PASSES),
+                    in_=scale_by_place[j, r],
                 )
 
         def load_plain():
@@ -127,12 +128,12 @@ def tile_lstmlayer_k_kernel(
             )
             for g in span:
                 raw[g, m] = x_raw[:, (g - span[0]) * GROUP_K : (g - span[0] + 1) * GROUP_K]
-            if m == {0: 2, 1: 3}.get(span[0], 1):
+            if m == (1 if len(span) > 1 else 2 if span[0] == 0 else 3):
                 for g in span:
                     if g % 2 == 0:
                         load_scales(g // 2)
                     load_w(g, 2 if g == 0 else PASSES)
-            if n == STEPS:
+            if n == PLAIN_LOAD:
                 load_plain()
 
         def sort_words(v):
@@ -184,11 +185,13 @@ def tile_lstmlayer_k_kernel(
                     stop=(g == GROUPS - 1 and s == PASSES - 1),
                 )
 
-        def compute_base():
+        def turn_plain():
             plain_turned = turn_pool.tile([P, 1 + 4, P], BF16, tag="turned")
             for a in range(1 + 4):
                 nc.tensor.transpose(plain_turned[:, a, :], plain_in[:, a, :], ident_bf16[:])
             nc.vector.tensor_copy(out=plain_t[:], in_=plain_turned[:])
+
+        def compute_base():
             base_sum = turn_pool.tile([P, GATE_COLS], F32, tag="turned")
             nc.tensor.matmul(
                 out=base_sum[:],
@@ -200,36 +203,42 @@ def tile_lstmlayer_k_kernel(
             nc.tensor.matmul(out=base_sum[:], lhsT=ones[:], rhs=bias_rows[:], start=False, stop=True)
             nc.vector.tensor_copy(out=base[:], in_=base_sum[:])
 
-        c_new = {}
+        in_forget = {}
+        candidate = {}
         out_gate = {}
+        tanh_c = {}
 
-        def cell_state(m):
+        def cell_gates(m):
             gates = cell_pool.tile([P, GATE_COLS], F32)
             for first in (0, 2 * HIDDEN):
                 cols = slice(first, first + 2 * HIDDEN)
                 nc.vector.tensor_add(out=gates[:, cols], in0=acc[m][:, cols], in1=base[:, cols])
-            in_forget = cell_pool.tile([P, 2 * HIDDEN], F32)
-            nc.scalar.activation(out=in_forget[:], in_=gates[:, 0 : 2 * HIDDEN], func=ACT.Sigmoid)
-            candidate = cell_pool.tile([P, HIDDEN], F32)
-            nc.scalar.activation(out=candidate[:], in_=gates[:, 2 * HIDDEN : 3 * HIDDEN], func=ACT.Tanh)
-            o_gate = cell_pool.tile([P, HIDDEN], F32)
-            nc.scalar.activation(out=o_gate[:], in_=gates[:, 3 * HIDDEN : 4 * HIDDEN], func=ACT.Sigmoid)
-            out_gate[m] = o_gate
+            i_f = cell_pool.tile([P, 2 * HIDDEN], F32)
+            nc.scalar.activation(out=i_f[:], in_=gates[:, 0 : 2 * HIDDEN], func=ACT.Sigmoid)
+            in_forget[m] = i_f
+            g_m = cell_pool.tile([P, HIDDEN], F32)
+            nc.scalar.activation(out=g_m[:], in_=gates[:, 2 * HIDDEN : 3 * HIDDEN], func=ACT.Tanh)
+            candidate[m] = g_m
+            o_m = cell_pool.tile([P, HIDDEN], F32)
+            nc.scalar.activation(out=o_m[:], in_=gates[:, 3 * HIDDEN : 4 * HIDDEN], func=ACT.Sigmoid)
+            out_gate[m] = o_m
+
+        def cell_state(m):
             kept = cell_pool.tile([P, HIDDEN], F32)
-            nc.vector.tensor_mul(out=kept[:], in0=in_forget[:, HIDDEN : 2 * HIDDEN], in1=c0_sb[:])
+            nc.vector.tensor_mul(out=kept[:], in0=in_forget[m][:, HIDDEN : 2 * HIDDEN], in1=c0_sb[:])
             fresh = cell_pool.tile([P, HIDDEN], F32)
-            nc.vector.tensor_mul(out=fresh[:], in0=in_forget[:, 0:HIDDEN], in1=candidate[:])
+            nc.vector.tensor_mul(out=fresh[:], in0=in_forget[m][:, 0:HIDDEN], in1=candidate[m][:])
             c_m = cell_pool.tile([P, HIDDEN], F32)
             nc.vector.tensor_add(out=c_m[:], in0=kept[:], in1=fresh[:])
-            c_new[m] = c_m
+            t_m = cell_pool.tile([P, HIDDEN], F32)
+            nc.scalar.activation(out=t_m[:], in_=c_m[:], func=ACT.Tanh)
+            tanh_c[m] = t_m
             if m == STEPS - 1:
                 nc.sync.dma_start(out=out_state[1], in_=c_m[:])
 
         def cell_output(m):
-            tanh_c = cell_pool.tile([P, HIDDEN], F32)
-            nc.scalar.activation(out=tanh_c[:], in_=c_new[m][:], func=ACT.Tanh)
             gated = cell_pool.tile([P, HIDDEN], F32)
-            nc.vector.tensor_mul(out=gated[:], in0=out_gate[m][:], in1=tanh_c[:])
+            nc.vector.tensor_mul(out=gated[:], in0=out_gate[m][:], in1=tanh_c[m][:])
             h_m = cell_pool.tile([P, HIDDEN], F32)
             nc.vector.tensor_add(out=h_m[:], in0=gated[:], in1=noise_sb[:])
             nc.sync.dma_start(out=out_h[m], in_=h_m[:])
@@ -242,23 +251,26 @@ def tile_lstmlayer_k_kernel(
             sort_words(v)
             transpose_unit(v)
         quantise(0)
-        sort_words(3)
         quantise(1)
         multiply(0)
-        transpose_unit(3)
-        sort_words(4)
-        quantise(2)
-        sort_words(5)
         multiply(1)
+        sort_words(3)
+        transpose_unit(3)
+        quantise(2)
+        sort_words(4)
+        sort_words(5)
 
         count = len(UNITS)
         finished = None
         for v in range(RUN, count, RUN):
             if v + 2 < count:
                 transpose_unit(v + 2)
-            quantise(v + 1)
-            if finished is not None:
-                cell_state(finished)
+            if v + 2 < count:
+                quantise(v + 1)
+            if finished is not None and finished >= 1:
+                cell_output(finished - 1)
+            if finished is not None and v + 4 < count:
+                cell_gates(finished)
             if v + 3 < count:
                 transpose_unit(v + 3)
             if v + 4 < count:
@@ -267,13 +279,22 @@ def tile_lstmlayer_k_kernel(
                 quantise(v + 2)
             if v + 5 < count:
                 sort_words(v + 5)
-            if finished is not None:
-                cell_output(finished)
+            if finished is not None and v + 4 >= count:
+                cell_gates(finished)
+            if v + 4 == count:
+                quantise(v + 3)
+            if finished is not None and v + 2 < count:
+                cell_state(finished)
             multiply(v)
             multiply(v + 1)
             g, m = UNITS[v + 1]
             finished = m if g == GROUPS - 1 else None
             if v + 1 == BASE_UNIT:
+                turn_plain()
+            if v + 1 == BASE_UNIT + RUN:
                 compute_base()
-        cell_state(finished)
-        cell_output(finished)
+        cell_gates(STEPS - 1)
+        cell_state(STEPS - 2)
+        cell_state(STEPS - 1)
+        cell_output(STEPS - 2)
+        cell_output(STEPS - 1)

@@ -29,7 +29,6 @@ SPAN_GROUPS = max(len(span) for span in SPANS)
 LOADS = [(span, m) for span in SPANS for m in range(STEPS)]
 UNITS = [(g, m) for span, m in LOADS for g in span]
 RAW_BUFS = 8
-RUN = 2
 PLAIN_LOAD = 20
 BASE_UNIT = 23
 
@@ -261,40 +260,26 @@ def tile_lstmlayer_k_kernel(
         sort_words(5)
 
         count = len(UNITS)
-        finished = None
-        for v in range(RUN, count, RUN):
+        last_unit = {UNITS.index((GROUPS - 1, m)): m for m in range(STEPS)}
+        for v in range(2, count):
             if v + 2 < count:
                 transpose_unit(v + 2)
-            if v + 2 < count:
+            if v + 1 < count:
                 quantise(v + 1)
-            if finished is not None and finished >= 1:
-                cell_output(finished - 1)
-            if finished is not None and v + 4 < count:
-                cell_gates(finished)
-            if v + 3 < count:
-                transpose_unit(v + 3)
             if v + 4 < count:
                 sort_words(v + 4)
-            if v + 2 < count:
-                quantise(v + 2)
-            if v + 5 < count:
-                sort_words(v + 5)
-            if finished is not None and v + 4 >= count:
-                cell_gates(finished)
-            if v + 4 == count:
-                quantise(v + 3)
-            if finished is not None and v + 2 < count:
-                cell_state(finished)
+            if v - 1 in last_unit:
+                cell_gates(last_unit[v - 1])
+            if v - 2 in last_unit:
+                cell_state(last_unit[v - 2])
+            if v - 3 in last_unit:
+                cell_output(last_unit[v - 3])
             multiply(v)
-            multiply(v + 1)
-            g, m = UNITS[v + 1]
-            finished = m if g == GROUPS - 1 else None
-            if v + 1 == BASE_UNIT:
+            if v == BASE_UNIT:
                 turn_plain()
-            if v + 1 == BASE_UNIT + RUN:
+            if v == BASE_UNIT + 1:
                 compute_base()
         cell_gates(STEPS - 1)
-        cell_state(STEPS - 2)
-        cell_state(STEPS - 1)
         cell_output(STEPS - 2)
+        cell_state(STEPS - 1)
         cell_output(STEPS - 1)

@@ -24,13 +24,14 @@ PASSES = 4
 GROUP_K = PASSES * K_PASS
 GROUPS = K // GROUP_K
 PLANE_PASSES = 8
-SPANS = [(0,), (1,), (2,), (3,), (4,), (5,), (6, 7)]
+SPANS = [(0,), (1,), (2, 3), (4, 5), (6, 7)]
 SPAN_GROUPS = max(len(span) for span in SPANS)
 LOADS = [(span, m) for span in SPANS for m in range(STEPS)]
 UNITS = [(g, m) for span, m in LOADS for g in span]
 RAW_BUFS = 8
-PLAIN_LOAD = 20
-BASE_UNIT = 23
+PLAIN_LOAD = 12
+RUN = 2
+BASE_UNIT = 19
 
 FLOPS = 2 * STEPS * P * GATE_COLS * K + 2 * P * GATE_COLS * HIDDEN
 
@@ -84,7 +85,8 @@ def tile_lstmlayer_k_kernel(
         ]
         base = const.tile([P, GATE_COLS], F32)
         plain_in = const.tile([P, 1 + 4, HIDDEN], BF16)
-        plain_t = const.tile([P, 1 + 4, P], BF16)
+        h0_t = const.tile([P, P], BF16)
+        w_hh_t = const.tile([P, P, 4], BF16)
         c0_sb = const.tile([P, HIDDEN], BF16)
         noise_sb = const.tile([P, HIDDEN], BF16)
         raw = {}
@@ -93,13 +95,9 @@ def tile_lstmlayer_k_kernel(
         x_codes = {}
         x_planes = {}
 
-        def load_w(g, passes):
-            for first in range(0, PASSES, passes):
-                some = slice(PASSES * g + first, PASSES * g + first + passes)
-                nc.sync.dma_start(
-                    out=w_codes[g][:, first : first + passes, :].bitcast(I32),
-                    in_=w_rows[some].rearrange("s p w -> p s w"),
-                )
+        def load_w(g):
+            for s in range(PASSES):
+                nc.sync.dma_start(out=w_codes[g][:, s, :].bitcast(I32), in_=w_rows[PASSES * g + s])
 
         def load_scales(j):
             for r in range(4):
@@ -112,7 +110,7 @@ def tile_lstmlayer_k_kernel(
 
         def load_plain():
             nc.sync.dma_start(out=plain_in[:, 0, :], in_=h0)
-            nc.sync.dma_start(out=plain_in[:, 1:5, :], in_=w_hh.rearrange("(a n) h -> n a h", n=P))
+            nc.sync.dma_start(out=plain_in[:, 1:5, :], in_=w_hh.rearrange("(n a) h -> n a h", a=4))
             nc.sync.dma_start(out=bias_rows[0:1, :], in_=b_ih.unsqueeze(0))
             nc.sync.dma_start(out=bias_rows[1:2, :], in_=b_hh.unsqueeze(0))
             nc.sync.dma_start(out=c0_sb[:], in_=c0)
@@ -131,7 +129,7 @@ def tile_lstmlayer_k_kernel(
                 for g in span:
                     if g % 2 == 0:
                         load_scales(g // 2)
-                    load_w(g, 2 if g == 0 else PASSES)
+                    load_w(g)
             if n == PLAIN_LOAD:
                 load_plain()
 
@@ -188,14 +186,15 @@ def tile_lstmlayer_k_kernel(
             plain_turned = turn_pool.tile([P, 1 + 4, P], BF16, tag="turned")
             for a in range(1 + 4):
                 nc.tensor.transpose(plain_turned[:, a, :], plain_in[:, a, :], ident_bf16[:])
-            nc.vector.tensor_copy(out=plain_t[:], in_=plain_turned[:])
+            nc.vector.tensor_copy(out=h0_t[:], in_=plain_turned[:, 0, :])
+            nc.vector.tensor_copy(out=w_hh_t[:], in_=plain_turned[:, 1:5, :].rearrange("h a n -> h n a"))
 
         def compute_base():
             base_sum = turn_pool.tile([P, GATE_COLS], F32, tag="turned")
             nc.tensor.matmul(
                 out=base_sum[:],
-                lhsT=plain_t[:, 0, :],
-                rhs=plain_t[:, 1:5, :].rearrange("h a n -> h (a n)"),
+                lhsT=h0_t[:],
+                rhs=w_hh_t[:].rearrange("h n a -> h (n a)"),
                 start=True,
                 stop=False,
             )
@@ -261,13 +260,28 @@ def tile_lstmlayer_k_kernel(
 
         count = len(UNITS)
         last_unit = {UNITS.index((GROUPS - 1, m)): m for m in range(STEPS)}
-        for v in range(2, count):
+        for v in range(RUN, count - 2 * RUN, RUN):
+            transpose_unit(v + 2)
+            quantise(v + 1)
+            if v - 1 in last_unit:
+                cell_gates(last_unit[v - 1])
+            transpose_unit(v + 3)
+            sort_words(v + 4)
+            quantise(v + 2)
+            sort_words(v + 5)
+            if v - 1 in last_unit:
+                cell_state(last_unit[v - 1])
+            multiply(v)
+            multiply(v + 1)
+            if v + 1 == BASE_UNIT:
+                turn_plain()
+            if v + 1 == BASE_UNIT + RUN:
+                compute_base()
+        for v in range(count - 2 * RUN, count):
             if v + 2 < count:
                 transpose_unit(v + 2)
             if v + 1 < count:
                 quantise(v + 1)
-            if v + 4 < count:
-                sort_words(v + 4)
             if v - 1 in last_unit:
                 cell_gates(last_unit[v - 1])
             if v - 2 in last_unit:
@@ -275,10 +289,6 @@ def tile_lstmlayer_k_kernel(
             if v - 3 in last_unit:
                 cell_output(last_unit[v - 3])
             multiply(v)
-            if v == BASE_UNIT:
-                turn_plain()
-            if v == BASE_UNIT + 1:
-                compute_base()
         cell_gates(STEPS - 1)
         cell_output(STEPS - 2)
         cell_state(STEPS - 1)

from contextlib import ExitStack

import concourse.mybir as mybir
from concourse.masks import make_identity

F32 = mybir.dt.float32
BF16 = mybir.dt.bfloat16
I32 = mybir.dt.int32
U32 = mybir.dt.uint32
U8 = mybir.dt.uint8
FP8X4 = mybir.dt.float8_e4m3fn_x4
ACT = mybir.ActivationFunctionType

P = 128
STEPS = 4
K = 16384
HIDDEN = 128
GATE_COLS = 4 * HIDDEN
PACK = 4
K_PASS = P * PACK
PAIRS = 2
BANK_PASSES = 2
PASSES = 4
GROUP_K = PASSES * K_PASS
GROUPS = K // GROUP_K
PLANE_PASSES = 8
SPANS = [(0,), (1,), (2, 3), (4, 5), (6, 7)]
SPAN_GROUPS = max(len(span) for span in SPANS)
LOADS = [(span, m) for span in SPANS for m in range(STEPS)]
UNITS = [(g, m) for span, m in LOADS for g in span]
RAW_BUFS = 8
PLAIN_LOAD = 12
RUN = 2
BASE_UNIT = 19

FLOPS = 2 * STEPS * P * GATE_COLS * K + 2 * P * GATE_COLS * HIDDEN


def tile_lstmlayer_k_kernel(
    tc, x, h0, c0, noise, w_words, w_scales, w_hh, b_ih, b_hh, out_h, out_state
):
    nc = tc.nc

    w_rows = w_words.rearrange("g p n t -> g p (n t)").bitcast(I32)
    scale_rows = w_scales.rearrange("g q n -> (g q) n").bitcast(I32)
    scale_by_place = scale_rows.rearrange("(j s a r) w -> j r a s w", s=PLANE_PASSES, a=4, r=4)

    with ExitStack() as ctx:
        const = ctx.enter_context(tc.tile_pool(name="const", bufs=1))
        raw_pool = ctx.enter_context(tc.tile_pool(name="raw", bufs=RAW_BUFS))
        sorted_pool = ctx.enter_context(tc.tile_pool(name="sorted", bufs=4))
        grouped_pool = ctx.enter_context(tc.tile_pool(name="grouped", bufs=3))
        codes_pool = ctx.enter_context(tc.tile_pool(name="codes", bufs=4))
        cell_pool = ctx.enter_context(tc.tile_pool(name="cell", bufs=2))
        acc_pool = ctx.enter_context(tc.psum_pool(name="acc", bufs=1))
        turn_pool = ctx.enter_context(tc.psum_pool(name="turn", bufs=4))
        ctx.enter_context(tc.manual_schedule())

        w_planes = [
            const.tile([P, PLANE_PASSES * GATE_COLS], U8, name="w_planes%d" % j, align_bytes=64)
            for j in range(GROUPS * PASSES // PLANE_PASSES)
        ]
        nc.vector.memset(w_planes[0][:].bitcast(I32), 0)
        ident_f32 = const.tile([P, P], F32)
        make_identity(nc, ident_f32[:])
        for plane in w_planes[1:]:
            nc.gpsimd.memset(plane[:].bitcast(I32), 0)
        ident_bf16 = const.tile([P, P], BF16)
        make_identity(nc, ident_bf16[:])
        bias_rows = const.tile([P, GATE_COLS], BF16)
        nc.gpsimd.memset(bias_rows[:], 0.0)
        ones = const.tile([P, P], BF16)
        nc.gpsimd.memset(ones[:], 1.0)
        table_in = const.tile([P, 1], F32)
        nc.vector.memset(table_in[:], 0.0)
        table_out = const.tile([P, 1], F32)
        nc.scalar.activation(out=table_out[:], in_=table_in[:], func=ACT.Sigmoid)

        w_codes = [
            const.tile([P, PASSES, GATE_COLS], U32, name="w_codes%d" % g, align_bytes=64)
            for g in range(GROUPS)
        ]
        acc = [
            acc_pool.tile([P, GATE_COLS], F32, name="acc%d" % m) for m in range(STEPS)
        ]
        base = const.tile([P, GATE_COLS], F32)
        plain_in = const.tile([P, 1 + 4, HIDDEN], BF16)
        h0_t = const.tile([P, P], BF16)
        w_hh_t = const.tile([P, P, 4], BF16)
        c0_sb = const.tile([P, HIDDEN], BF16)
        noise_sb = const.tile([P, HIDDEN], BF16)
        raw = {}
        in_order = {}
        grouped = {}
        x_codes = {}
        x_planes = {}

        def load_w(g):
            for s in range(PASSES):
                nc.sync.dma_start(out=w_codes[g][:, s, :].bitcast(I32), in_=w_rows[PASSES * g + s])

        def load_scales(j):
            for r in range(4):
                nc.sync.dma_start(
                    out=w_planes[j][4 * j + r : P : 32, :]
                    .bitcast(I32)
                    .rearrange("a (s w) -> a s w", s=PLANE_PASSES),
                    in_=scale_by_place[j, r],
                )

        def load_plain():
            nc.sync.dma_start(out=plain_in[:, 0, :], in_=h0)
            nc.sync.dma_start(out=plain_in[:, 1:5, :], in_=w_hh.rearrange("(n a) h -> n a h", a=4))
            nc.sync.dma_start(out=bias_rows[0:1, :], in_=b_ih.unsqueeze(0))
            nc.sync.dma_start(out=bias_rows[1:2, :], in_=b_hh.unsqueeze(0))
            nc.sync.dma_start(out=c0_sb[:], in_=c0)
            nc.sync.dma_start(out=noise_sb[:], in_=noise)

        def load(n):
            span, m = LOADS[n]
            x_raw = raw_pool.tile([P, SPAN_GROUPS * GROUP_K], BF16)
            width = len(span) * GROUP_K
            nc.sync.dma_start(
                out=x_raw[:, :width], in_=x[m, :, span[0] * GROUP_K : span[0] * GROUP_K + width]
            )
            for g in span:
                raw[g, m] = x_raw[:, (g - span[0]) * GROUP_K : (g - span[0] + 1) * GROUP_K]
            if m == (1 if len(span) > 1 else 2 if span[0] == 0 else 3):
                for g in span:
                    if g % 2 == 0:
                        load_scales(g // 2)
                    load_w(g)
            if n == PLAIN_LOAD:
                load_plain()

        def sort_words(v):
            g, m = UNITS[v]
            x_sorted = sorted_pool.tile([P, PASSES, PAIRS, P], F32)
            in_order[v] = x_sorted
            nc.vector.tensor_copy(
                out=x_sorted[:],
                in_=raw[g, m].bitcast(F32).rearrange("b (s p u) -> b s u p", s=PASSES, p=P),
            )
            done = [n for n in range(len(LOADS)) if LOADS[n][1] == m and LOADS[n][0][-1] == g]
            for n in done:
                if n + RAW_BUFS < len(LOADS):
                    load(n + RAW_BUFS)

        def transpose_unit(v):
            x_grouped = grouped_pool.tile([P, PASSES * K_PASS], BF16, align_bytes=64)
            grouped[v] = x_grouped
            grouped_words = x_grouped[:].bitcast(F32).rearrange("p (s b u) -> p s b u", s=PASSES, u=PAIRS)
            for first in range(0, PASSES, BANK_PASSES):
                turned = turn_pool.tile([P, BANK_PASSES, PAIRS, P], F32, tag="turned")
                for s in range(BANK_PASSES):
                    for u in range(PAIRS):
                        nc.tensor.transpose(turned[:, s, u, :], in_order[v][:, first + s, u, :], ident_f32[:])
                nc.scalar.copy(
                    out=grouped_words[:, first : first + BANK_PASSES],
                    in_=turned[:].rearrange("p s u b -> p s b u"),
                )

        def quantise(v):
            codes = codes_pool.tile([P, PASSES * P], U32, align_bytes=64)
            x_codes[v] = codes
            plane = codes_pool.tile([P, PASSES * P], U8, align_bytes=64)
            x_planes[v] = plane
            nc.vector.quantize_mx(out=codes[:].bitcast(FP8X4), scales=plane[:], in_=grouped[v][:])

        def multiply(v):
            g, m = UNITS[v]
            for s in range(PASSES):
                rows = slice(s * P, (s + 1) * P)
                j, slot = divmod(g * PASSES + s, PLANE_PASSES)
                nc.tensor.matmul_mx(
                    out=acc[m][:],
                    lhsT=x_codes[v][:, rows].bitcast(FP8X4),
                    lhsT_scale=x_planes[v][:, rows],
                    rhs=w_codes[g][:, s, :].bitcast(FP8X4),
                    rhs_scale=w_planes[j][4 * j : P, slot * GATE_COLS : (slot + 1) * GATE_COLS],
                    start=(g == 0 and s == 0),
                    stop=(g == GROUPS - 1 and s == PASSES - 1),
                )

        def turn_plain():
            plain_turned = turn_pool.tile([P, 1 + 4, P], BF16, tag="turned")
            for a in range(1 + 4):
                nc.tensor.transpose(plain_turned[:, a, :], plain_in[:, a, :], ident_bf16[:])
            nc.vector.tensor_copy(out=h0_t[:], in_=plain_turned[:, 0, :])
            nc.vector.tensor_copy(out=w_hh_t[:], in_=plain_turned[:, 1:5, :].rearrange("h a n -> h n a"))

        def compute_base():
            base_sum = turn_pool.tile([P, GATE_COLS], F32, tag="turned")
            nc.tensor.matmul(
                out=base_sum[:],
                lhsT=h0_t[:],
                rhs=w_hh_t[:].rearrange("h n a -> h (n a)"),
                start=True,
                stop=False,
            )
            nc.tensor.matmul(out=base_sum[:], lhsT=ones[:], rhs=bias_rows[:], start=False, stop=True)
            nc.vector.tensor_copy(out=base[:], in_=base_sum[:])

        in_forget = {}
        candidate = {}
        out_gate = {}
        tanh_c = {}

        def cell_gates(m):
            gates = cell_pool.tile([P, GATE_COLS], F32)
            for first in (0, 2 * HIDDEN):
                cols = slice(first, first + 2 * HIDDEN)
                nc.vector.tensor_add(out=gates[:, cols], in0=acc[m][:, cols], in1=base[:, cols])
            i_f = cell_pool.tile([P, 2 * HIDDEN], F32)
            nc.scalar.activation(out=i_f[:], in_=gates[:, 0 : 2 * HIDDEN], func=ACT.Sigmoid)
            in_forget[m] = i_f
            g_m = cell_pool.tile([P, HIDDEN], F32)
            nc.scalar.activation(out=g_m[:], in_=gates[:, 2 * HIDDEN : 3 * HIDDEN], func=ACT.Tanh)
            candidate[m] = g_m
            o_m = cell_pool.tile([P, HIDDEN], F32)
            nc.scalar.activation(out=o_m[:], in_=gates[:, 3 * HIDDEN : 4 * HIDDEN], func=ACT.Sigmoid)
            out_gate[m] = o_m

        def cell_state(m):
            kept = cell_pool.tile([P, HIDDEN], F32)
            nc.vector.tensor_mul(out=kept[:], in0=in_forget[m][:, HIDDEN : 2 * HIDDEN], in1=c0_sb[:])
            fresh = cell_pool.tile([P, HIDDEN], F32)
            nc.vector.tensor_mul(out=fresh[:], in0=in_forget[m][:, 0:HIDDEN], in1=candidate[m][:])
            c_m = cell_pool.tile([P, HIDDEN], F32)
            nc.vector.tensor_add(out=c_m[:], in0=kept[:], in1=fresh[:])
            t_m = cell_pool.tile([P, HIDDEN], F32)
            nc.scalar.activation(out=t_m[:], in_=c_m[:], func=ACT.Tanh)
            tanh_c[m] = t_m
            if m == STEPS - 1:
                nc.sync.dma_start(out=out_state[1], in_=c_m[:])

        def cell_output(m):
            gated = cell_pool.tile([P, HIDDEN], F32)
            nc.vector.tensor_mul(out=gated[:], in0=out_gate[m][:], in1=tanh_c[m][:])
            h_m = cell_pool.tile([P, HIDDEN], F32)
            nc.vector.tensor_add(out=h_m[:], in0=gated[:], in1=noise_sb[:])
            nc.sync.dma_start(out=out_h[m], in_=h_m[:])
            if m == STEPS - 1:
                nc.sync.dma_start(out=out_state[0], in_=h_m[:])

        for n in range(RAW_BUFS):
            load(n)
        for v in range(3):
            sort_words(v)
            transpose_unit(v)
        quantise(0)
        quantise(1)
        multiply(0)
        multiply(1)
        sort_words(3)
        transpose_unit(3)
        quantise(2)
        sort_words(4)
        sort_words(5)

        count = len(UNITS)
        last_unit = {UNITS.index((GROUPS - 1, m)): m for m in range(STEPS)}
        for v in range(RUN, count - 2 * RUN, RUN):
            transpose_unit(v + 2)
            quantise(v + 1)
            if v - 1 in last_unit:
                cell_gates(last_unit[v - 1])
            transpose_unit(v + 3)
            sort_words(v + 4)
            quantise(v + 2)
            sort_words(v + 5)
            if v - 1 in last_unit:
                cell_state(last_unit[v - 1])
            multiply(v)
            multiply(v + 1)
            if v + 1 == BASE_UNIT:
                turn_plain()
            if v + 1 == BASE_UNIT + RUN:
                compute_base()
        for v in range(count - 2 * RUN, count):
            if v + 2 < count:
                transpose_unit(v + 2)
            if v + 1 < count:
                quantise(v + 1)
            if v - 1 in last_unit:
                cell_gates(last_unit[v - 1])
            if v - 2 in last_unit:
                cell_state(last_unit[v - 2])
            if v - 3 in last_unit:
                cell_output(last_unit[v - 3])
            multiply(v)
        cell_gates(STEPS - 1)
        cell_output(STEPS - 2)
        cell_state(STEPS - 1)
        cell_output(STEPS - 1)
